import numpy as np
import ml_dtypes


def mxq(x, axis, fmt="e4m3"):
    dtype, down = {"e4m3": (ml_dtypes.float8_e4m3fn, 7), "e5m2": (ml_dtypes.float8_e5m2, 14)}[fmt]
    v = np.moveaxis(np.asarray(x, np.float32).astype(ml_dtypes.bfloat16).astype(np.float64), axis, -1)
    blocks = v.reshape(v.shape[:-1] + (-1, 32))
    amax = np.abs(blocks).max(-1, keepdims=True)
    byte = np.maximum(np.where(amax > 0, np.frexp(amax)[1] - 1 + 127, 0) - down, 1)
    scale = np.exp2(byte - 127.0)
    codes = (blocks / scale).astype(np.float32).astype(dtype).astype(np.float64)
    return np.moveaxis((codes * scale).reshape(v.shape), -1, axis)


WIDE = False


def mx_kscale(k):
    if not WIDE:
        return np.ones(k)
    levels = np.array([10, -10, 5, -5, 0])
    a = np.random.permutation(np.resize(levels, k // 512 * 4)).reshape(k // 512, 4)
    idx = np.arange(k)
    return np.exp2(a[idx // 512, idx % 128 // 32])


BF16 = ml_dtypes.bfloat16


def bf(x):
    return np.asarray(x, np.float32).astype(BF16)


def f64(x):
    return np.asarray(x).astype(np.float64)


BATCH, SEQ, IN_DIM, MID_DIM, OUT_DIM = 2, 64, 1024, 1024, 512
CB = 2.0 ** -np.round(np.log2(IN_DIM) / 2)
CA = 2.0 ** -np.round(np.log2(MID_DIM) / 2)


def signs(shape):
    return np.where(np.random.standard_normal(shape) >= 0, 1.0, -1.0)


def setup_inputs():
    s, t = mx_kscale(IN_DIM), mx_kscale(MID_DIM)
    return {"x": bf(np.random.standard_normal((BATCH, SEQ, IN_DIM)) * s),
            "scaling0": bf(0.5 + np.random.uniform(size=IN_DIM)),
            "B": bf(signs((MID_DIM, IN_DIM)) * CB / s[None, :]),
            "scaling2": bf((0.5 + np.random.uniform(size=MID_DIM)) * t),
            "A": bf(signs((OUT_DIM, MID_DIM)) * CA / t[None, :]),
            "scaling4": bf(0.5 + np.random.uniform(size=OUT_DIM)),
            "bias": bf(np.random.standard_normal(OUT_DIM))}


def reference(x, scaling0, B, scaling2, A, scaling4, bias):
    h = f64(x) * f64(scaling0)
    h = mxq(h, 2, "e4m3") @ mxq(f64(B), 1, "e4m3").T
    h = h * f64(scaling2)
    h = mxq(h, 2, "e4m3") @ mxq(f64(A), 1, "e4m3").T
    return h * f64(scaling4) + f64(bias)

@@ -1,0 +1,206 @@
+from contextlib import ExitStack
+
+import concourse.mybir as mybir
+from concourse.masks import make_identity
+
+BF16 = mybir.dt.bfloat16
+F32 = mybir.dt.float32
+U32 = mybir.dt.uint32
+U8 = mybir.dt.uint8
+FP8X4 = mybir.dt.float8_e4m3fn_x4
+MULT = mybir.AluOpType.mult
+ADD = mybir.AluOpType.add
+
+P = 128
+PACK = 4
+PASSES = 2
+K_DIM = 1024
+OUT_DIM = 512
+WORD_BLOCKS = 4
+CHUNK_ROWS = 2 * P
+B_CHUNKS = 4
+A_CHUNKS = 2
+TILE_WORDS = PASSES * P
+
+FLOPS = 2 * P * K_DIM * K_DIM + 2 * P * K_DIM * OUT_DIM
+
+
+def pass_cols(g):
+    return slice(g * P, (g + 1) * P)
+
+
+def transpose_row_tile(nc, banks, rows, identity):
+    words = rows.bitcast(F32)
+    bank = banks.tile([P, WORD_BLOCKS, P], F32, name="bank")
+    for j in range(WORD_BLOCKS):
+        nc.tensor.transpose(bank[:, j, :], words[:, j * P : (j + 1) * P], identity[:])
+    return bank
+
+
+def tile_doublebinarylinear_s_kernel(tc, x, scaling0, B, scaling2, A, scaling4, bias, out):
+    nc = tc.nc
+    x_rows = x.rearrange("b s k -> (b s) k")
+    out_rows = out.rearrange("b s o -> (b s) o")
+    chunk_rows = [B[c * CHUNK_ROWS : (c + 1) * CHUNK_ROWS, :] for c in range(B_CHUNKS)]
+    chunk_rows += [A[c * CHUNK_ROWS : (c + 1) * CHUNK_ROWS, :] for c in range(A_CHUNKS)]
+    chunks = len(chunk_rows)
+
+    with ExitStack() as ctx:
+        keep = ctx.enter_context(tc.tile_pool(name="keep", bufs=1))
+        stage = ctx.enter_context(tc.tile_pool(name="stage", bufs=4))
+        banks = ctx.enter_context(tc.psum_pool(name="banks", bufs=4))
+        sums = ctx.enter_context(tc.psum_pool(name="sums", bufs=1))
+
+        identity = keep.tile([P, P], F32)
+        make_identity(nc, identity[:])
+        ones = keep.tile([P, P], BF16)
+        nc.vector.memset(ones[:], 1.0)
+        vector_rows = keep.tile([P, P], F32)
+        nc.vector.memset(vector_rows[:], 0.0)
+        row_zero = keep.tile([P, 2 * OUT_DIM], BF16)
+        nc.vector.memset(row_zero[:].bitcast(F32), 0.0)
+
+        x_sb = keep.tile([P, K_DIM], BF16)
+        nc.sync.dma_start(out=x_sb[:], in_=x_rows)
+        w_sb = []
+        for i in range(chunks):
+            chunk = keep.tile([P, 2, K_DIM], BF16, name="w_sb%d" % i)
+            nc.sync.dma_start(out=chunk[:], in_=chunk_rows[i].rearrange("(p e) k -> p e k", e=2))
+            w_sb.append(chunk)
+        vector_halves = vector_rows[:].bitcast(BF16)
+        nc.scalar.dma_start(
+            out=vector_halves[0:WORD_BLOCKS, :], in_=scaling0.rearrange("(j w) -> j w", j=WORD_BLOCKS)
+        )
+        nc.scalar.dma_start(
+            out=vector_halves[WORD_BLOCKS : 2 * WORD_BLOCKS, :],
+            in_=scaling2.rearrange("(j w) -> j w", j=WORD_BLOCKS),
+        )
+        nc.scalar.dma_start(out=row_zero[0:1, 0:OUT_DIM], in_=scaling4.unsqueeze(0))
+        nc.scalar.dma_start(out=row_zero[0:1, OUT_DIM : 2 * OUT_DIM], in_=bias.unsqueeze(0))
+
+        vector_bank = banks.tile([P, WORD_BLOCKS, P], F32, name="bank")
+        nc.tensor.transpose(vector_bank[:, 0, :], vector_rows[:], identity[:])
+        scale_words = keep.tile([P, 2 * WORD_BLOCKS], F32)
+        nc.vector.tensor_copy(out=scale_words[:], in_=vector_bank[:, 0, 0 : 2 * WORD_BLOCKS])
+        scale_cols = scale_words[:].bitcast(BF16)
+        s0_cols = scale_cols[:, 0 : 2 * WORD_BLOCKS]
+        s2_cols = scale_cols[:, 2 * WORD_BLOCKS : 4 * WORD_BLOCKS]
+
+        x_bank = transpose_row_tile(nc, banks, x_sb[:], identity)
+        x_halves = x_bank[:].bitcast(BF16)
+        h0_grouped = keep.tile([P, PASSES, P, PACK], BF16, align_bytes=64)
+        for g in range(PASSES):
+            nc.vector.tensor_tensor(
+                out=h0_grouped[:, g].rearrange("p r (u e) -> p r u e", e=2),
+                in0=x_halves[:, 2 * g : 2 * g + 2, :].rearrange("p u (r e) -> p r u e", e=2),
+                in1=s0_cols[:, PACK * g : PACK * (g + 1)]
+                .rearrange("p (u e) -> p u e", e=2)
+                .unsqueeze(1)
+                .to_broadcast([P, P, 2, 2]),
+                op=MULT,
+            )
+        h0_codes = keep.tile([P, TILE_WORDS], U32, align_bytes=64)
+        h0_scales = keep.tile([P, TILE_WORDS], U8, align_bytes=64)
+        nc.vector.quantize_mx(
+            out=h0_codes[:].bitcast(FP8X4),
+            scales=h0_scales[:],
+            in_=h0_grouped[:].rearrange("p g r t -> p (g r t)"),
+        )
+
+        spread = []
+        for v in range(2):
+            spread_bank = banks.tile([P, WORD_BLOCKS, P], F32, name="bank")
+            nc.tensor.matmul(
+                out=spread_bank[:].rearrange("p a b -> p (a b)"),
+                lhsT=ones[:],
+                rhs=row_zero[:, v * OUT_DIM : (v + 1) * OUT_DIM],
+                start=True,
+                stop=True,
+            )
+            spread_sb = keep.tile([P, OUT_DIM], F32, name="spread%d" % v)
+            nc.scalar.copy(out=spread_sb[:], in_=spread_bank[:].rearrange("p a b -> p (a b)"))
+            spread.append(spread_sb)
+        s4_all, bias_all = spread
+
+        w_codes = [keep.tile([P, 2, TILE_WORDS], U32, name="w_codes%d" % i, align_bytes=64) for i in range(chunks)]
+        w_scales = [keep.tile([P, 2, TILE_WORDS], U8, name="w_scales%d" % i, align_bytes=64) for i in range(chunks)]
+        h1 = [sums.tile([P, PACK, P], F32, name="h1_%d" % g) for g in range(PASSES)]
+        h3 = [sums.tile([P, 2, P], F32, name="h3_%d" % c) for c in range(A_CHUNKS)]
+        h2_codes = keep.tile([P, TILE_WORDS], U32, align_bytes=64)
+        h2_scales = keep.tile([P, TILE_WORDS], U8, align_bytes=64)
+
+        def quantise_chunk(i):
+            for e in range(2):
+                bank = transpose_row_tile(nc, banks, w_sb[i][:, e, :], identity)
+                grouped = stage.tile([P, PASSES, P, PACK], BF16, align_bytes=64)
+                nc.scalar.copy(
+                    out=grouped[:].bitcast(F32), in_=bank[:].rearrange("p (g u) r -> p g r u", u=2)
+                )
+                nc.vector.quantize_mx(
+                    out=w_codes[i][:, e, :].bitcast(FP8X4),
+                    scales=w_scales[i][:, e, :],
+                    in_=grouped[:].rearrange("p g r t -> p (g r t)"),
+                )
+
+        def first_matmul(c):
+            g2, u2 = divmod(c, 2)
+            for e in range(2):
+                for g in range(PASSES):
+                    nc.tensor.matmul_mx(
+                        out=h1[g2][:, 2 * u2 + e, :],
+                        lhsT=w_codes[c][:, e, pass_cols(g)].bitcast(FP8X4),
+                        lhsT_scale=w_scales[c][:, e, pass_cols(g)],
+                        rhs=h0_codes[:, pass_cols(g)].bitcast(FP8X4),
+                        rhs_scale=h0_scales[:, pass_cols(g)],
+                        start=(g == 0),
+                        stop=(g == PASSES - 1),
+                    )
+            if u2 == 1:
+                h2_grouped = stage.tile([P, P, PACK], BF16, align_bytes=64)
+                nc.vector.tensor_tensor(
+                    out=h2_grouped[:],
+                    in0=h1[g2][:].rearrange("p t r -> p r t"),
+                    in1=s2_cols[:, PACK * g2 : PACK * (g2 + 1)].unsqueeze(1).to_broadcast([P, P, PACK]),
+                    op=MULT,
+                )
+                nc.vector.quantize_mx(
+                    out=h2_codes[:, pass_cols(g2)].bitcast(FP8X4),
+                    scales=h2_scales[:, pass_cols(g2)],
+                    in_=h2_grouped[:].rearrange("p r t -> p (r t)"),
+                )
+
+        def second_matmul(c):
+            i = B_CHUNKS + c
+            for e in range(2):
+                for g in range(PASSES):
+                    nc.tensor.matmul_mx(
+                        out=h3[c][:, e, :],
+                        lhsT=h2_codes[:, pass_cols(g)].bitcast(FP8X4),
+                        lhsT_scale=h2_scales[:, pass_cols(g)],
+                        rhs=w_codes[i][:, e, pass_cols(g)].bitcast(FP8X4),
+                        rhs_scale=w_scales[i][:, e, pass_cols(g)],
+                        start=(g == 0),
+                        stop=(g == PASSES - 1),
+                    )
+            cols = slice(c * CHUNK_ROWS, (c + 1) * CHUNK_ROWS)
+            result = stage.tile([P, CHUNK_ROWS], F32)
+            nc.vector.tensor_tensor(
+                out=result[:].rearrange("r (p e) -> r p e", e=2),
+                in0=h3[c][:].rearrange("r e p -> r p e"),
+                in1=s4_all[:, cols].rearrange("r (p e) -> r p e", e=2),
+                op=MULT,
+            )
+            nc.vector.tensor_tensor(out=result[:], in0=result[:], in1=bias_all[:, cols], op=ADD)
+            nc.sync.dma_start(out=out_rows[:, cols], in_=result[:])
+
+        def multiply_chunk(i):
+            if i < B_CHUNKS:
+                first_matmul(i)
+            else:
+                second_matmul(i - B_CHUNKS)
+
+        quantise_chunk(0)
+        for i in range(1, chunks):
+            quantise_chunk(i)
+            multiply_chunk(i - 1)
+        multiply_chunk(chunks - 1)

@@ -48,43 +48,33 @@ def tile_doublebinarylinear_s_kernel(tc, x, scaling0, B, scaling2, A, scaling4, 
     with ExitStack() as ctx:
         keep = ctx.enter_context(tc.tile_pool(name="keep", bufs=1))
         stage = ctx.enter_context(tc.tile_pool(name="stage", bufs=4))
-        banks = ctx.enter_context(tc.psum_pool(name="banks", bufs=4))
+        banks = ctx.enter_context(tc.psum_pool(name="banks", bufs=5))
         sums = ctx.enter_context(tc.psum_pool(name="sums", bufs=1))
+        ctx.enter_context(tc.manual_schedule())
 
         identity = keep.tile([P, P], F32)
         make_identity(nc, identity[:])
         ones = keep.tile([P, P], BF16)
         nc.vector.memset(ones[:], 1.0)
-        vector_rows = keep.tile([P, P], F32)
-        nc.vector.memset(vector_rows[:], 0.0)
         row_zero = keep.tile([P, 2 * OUT_DIM], BF16)
         nc.vector.memset(row_zero[:].bitcast(F32), 0.0)
 
+        s0_cols = keep.tile([P, 2 * WORD_BLOCKS], BF16)
+        s2_cols = keep.tile([P, 2 * WORD_BLOCKS], BF16)
+        for s_cols, scaling in ((s0_cols, scaling0), (s2_cols, scaling2)):
+            nc.scalar.dma_start(
+                out=s_cols[:].rearrange("p (j e) -> p j e", e=2),
+                in_=scaling.rearrange("(j p e) -> p j e", p=P, e=2),
+            )
         x_sb = keep.tile([P, K_DIM], BF16)
         nc.sync.dma_start(out=x_sb[:], in_=x_rows)
+        nc.sync.dma_start(out=row_zero[0:1, 0:OUT_DIM], in_=scaling4.unsqueeze(0))
+        nc.sync.dma_start(out=row_zero[0:1, OUT_DIM : 2 * OUT_DIM], in_=bias.unsqueeze(0))
         w_sb = []
         for i in range(chunks):
             chunk = keep.tile([P, 2, K_DIM], BF16, name="w_sb%d" % i)
             nc.sync.dma_start(out=chunk[:], in_=chunk_rows[i].rearrange("(p e) k -> p e k", e=2))
             w_sb.append(chunk)
-        vector_halves = vector_rows[:].bitcast(BF16)
-        nc.scalar.dma_start(
-            out=vector_halves[0:WORD_BLOCKS, :], in_=scaling0.rearrange("(j w) -> j w", j=WORD_BLOCKS)
-        )
-        nc.scalar.dma_start(
-            out=vector_halves[WORD_BLOCKS : 2 * WORD_BLOCKS, :],
-            in_=scaling2.rearrange("(j w) -> j w", j=WORD_BLOCKS),
-        )
-        nc.scalar.dma_start(out=row_zero[0:1, 0:OUT_DIM], in_=scaling4.unsqueeze(0))
-        nc.scalar.dma_start(out=row_zero[0:1, OUT_DIM : 2 * OUT_DIM], in_=bias.unsqueeze(0))
-
-        vector_bank = banks.tile([P, WORD_BLOCKS, P], F32, name="bank")
-        nc.tensor.transpose(vector_bank[:, 0, :], vector_rows[:], identity[:])
-        scale_words = keep.tile([P, 2 * WORD_BLOCKS], F32)
-        nc.vector.tensor_copy(out=scale_words[:], in_=vector_bank[:, 0, 0 : 2 * WORD_BLOCKS])
-        scale_cols = scale_words[:].bitcast(BF16)
-        s0_cols = scale_cols[:, 0 : 2 * WORD_BLOCKS]
-        s2_cols = scale_cols[:, 2 * WORD_BLOCKS : 4 * WORD_BLOCKS]
 
         x_bank = transpose_row_tile(nc, banks, x_sb[:], identity)
         x_halves = x_bank[:].bitcast(BF16)
@@ -107,25 +97,19 @@ def tile_doublebinarylinear_s_kernel(tc, x, scaling0, B, scaling2, A, scaling4, 
             in_=h0_grouped[:].rearrange("p g r t -> p (g r t)"),
         )
 
-        spread = []
-        for v in range(2):
-            spread_bank = banks.tile([P, WORD_BLOCKS, P], F32, name="bank")
-            nc.tensor.matmul(
-                out=spread_bank[:].rearrange("p a b -> p (a b)"),
-                lhsT=ones[:],
-                rhs=row_zero[:, v * OUT_DIM : (v + 1) * OUT_DIM],
-                start=True,
-                stop=True,
-            )
-            spread_sb = keep.tile([P, OUT_DIM], F32, name="spread%d" % v)
-            nc.scalar.copy(out=spread_sb[:], in_=spread_bank[:].rearrange("p a b -> p (a b)"))
-            spread.append(spread_sb)
-        s4_all, bias_all = spread
+        s4_bank = banks.tile([P, WORD_BLOCKS, P], F32, name="bank")
+        s4_spread = s4_bank[:].rearrange("p a b -> p (a b)")
+        nc.tensor.matmul(out=s4_spread, lhsT=ones[:], rhs=row_zero[:, 0:OUT_DIM], start=True, stop=True)
+        s4_all = keep.tile([P, OUT_DIM], F32)
+        nc.scalar.copy(out=s4_all[:], in_=s4_spread)
+        bias_all = sums.tile([P, OUT_DIM], F32)
+        nc.tensor.matmul(
+            out=bias_all[:], lhsT=ones[:], rhs=row_zero[:, OUT_DIM : 2 * OUT_DIM], start=True, stop=True
+        )
 
         w_codes = [keep.tile([P, 2, TILE_WORDS], U32, name="w_codes%d" % i, align_bytes=64) for i in range(chunks)]
         w_scales = [keep.tile([P, 2, TILE_WORDS], U8, name="w_scales%d" % i, align_bytes=64) for i in range(chunks)]
-        h1 = [sums.tile([P, PACK, P], F32, name="h1_%d" % g) for g in range(PASSES)]
-        h3 = [sums.tile([P, 2, P], F32, name="h3_%d" % c) for c in range(A_CHUNKS)]
+        h1 = [sums.tile([P, PACK, P], F32, name="h1_%d" % g, tag="sum%d" % g) for g in range(PASSES)]
         h2_codes = keep.tile([P, TILE_WORDS], U32, align_bytes=64)
         h2_scales = keep.tile([P, TILE_WORDS], U8, align_bytes=64)
 
@@ -171,10 +155,11 @@ def tile_doublebinarylinear_s_kernel(tc, x, scaling0, B, scaling2, A, scaling4, 
 
         def second_matmul(c):
             i = B_CHUNKS + c
+            h3 = sums.tile([P, 2, P], F32, tag="sum%d" % c)
             for e in range(2):
                 for g in range(PASSES):
                     nc.tensor.matmul_mx(
-                        out=h3[c][:, e, :],
+                        out=h3[:, e, :],
                         lhsT=h2_codes[:, pass_cols(g)].bitcast(FP8X4),
                         lhsT_scale=h2_scales[:, pass_cols(g)],
                         rhs=w_codes[i][:, e, pass_cols(g)].bitcast(FP8X4),
@@ -186,7 +171,7 @@ def tile_doublebinarylinear_s_kernel(tc, x, scaling0, B, scaling2, A, scaling4, 
             result = stage.tile([P, CHUNK_ROWS], F32)
             nc.vector.tensor_tensor(
                 out=result[:].rearrange("r (p e) -> r p e", e=2),
-                in0=h3[c][:].rearrange("r e p -> r p e"),
+                in0=h3[:].rearrange("r e p -> r p e"),
                 in1=s4_all[:, cols].rearrange("r (p e) -> r p e", e=2),
                 op=MULT,
             )

@@ -21,6 +21,7 @@ CHUNK_ROWS = 2 * P
 B_CHUNKS = 4
 A_CHUNKS = 2
 TILE_WORDS = PASSES * P
+WARM_PASSES = 12
 
 FLOPS = 2 * P * K_DIM * K_DIM + 2 * P * K_DIM * OUT_DIM
 
@@ -54,10 +55,28 @@ def tile_doublebinarylinear_s_kernel(tc, x, scaling0, B, scaling2, A, scaling4, 
 
         identity = keep.tile([P, P], F32)
         make_identity(nc, identity[:])
-        ones = keep.tile([P, P], BF16)
-        nc.vector.memset(ones[:], 1.0)
         row_zero = keep.tile([P, 2 * OUT_DIM], BF16)
         nc.vector.memset(row_zero[:].bitcast(F32), 0.0)
+
+        warm_zeros = keep.tile([P, PACK * P], BF16, align_bytes=64)
+        nc.vector.memset(warm_zeros[:].bitcast(F32), 0.0)
+        warm_codes = keep.tile([P, P], U32, align_bytes=64)
+        warm_scales = keep.tile([P, P], U8, align_bytes=64)
+        nc.vector.quantize_mx(out=warm_codes[:].bitcast(FP8X4), scales=warm_scales[:], in_=warm_zeros[:])
+        warm_bank = banks.tile([P, WORD_BLOCKS, P], F32, name="bank")
+        for w in range(WARM_PASSES):
+            nc.tensor.matmul_mx(
+                out=warm_bank[:, 0, :],
+                lhsT=warm_codes[:].bitcast(FP8X4),
+                lhsT_scale=warm_scales[:],
+                rhs=warm_codes[:].bitcast(FP8X4),
+                rhs_scale=warm_scales[:],
+                start=(w == 0),
+                stop=(w == WARM_PASSES - 1),
+            )
+
+        ones = keep.tile([P, P], BF16)
+        nc.vector.memset(ones[:], 1.0)
 
         s0_cols = keep.tile([P, 2 * WORD_BLOCKS], BF16)
         s2_cols = keep.tile([P, 2 * WORD_BLOCKS], BF16)

@@ -21,6 +21,8 @@ CHUNK_ROWS = 2 * P
 B_CHUNKS = 4
 A_CHUNKS = 2
 TILE_WORDS = PASSES * P
+CHUNK_PASSES = 2 * PASSES
+LOOKAHEAD = 2
 WARM_PASSES = 12
 
 FLOPS = 2 * P * K_DIM * K_DIM + 2 * P * K_DIM * OUT_DIM
@@ -49,32 +51,35 @@ def tile_doublebinarylinear_s_kernel(tc, x, scaling0, B, scaling2, A, scaling4, 
     with ExitStack() as ctx:
         keep = ctx.enter_context(tc.tile_pool(name="keep", bufs=1))
         stage = ctx.enter_context(tc.tile_pool(name="stage", bufs=4))
-        banks = ctx.enter_context(tc.psum_pool(name="banks", bufs=5))
+        banks = ctx.enter_context(tc.psum_pool(name="banks", bufs=4))
         sums = ctx.enter_context(tc.psum_pool(name="sums", bufs=1))
         ctx.enter_context(tc.manual_schedule())
+
+        zeros = keep.tile([P, PACK * P], BF16, align_bytes=64)
+        nc.vector.memset(zeros[:].bitcast(F32), 0.0)
+        zero_codes = keep.tile([P, P], U32, align_bytes=64)
+        zero_scales = keep.tile([P, P], U8, align_bytes=64)
+        nc.vector.quantize_mx(out=zero_codes[:].bitcast(FP8X4), scales=zero_scales[:], in_=zeros[:])
+        idle_sums = sums.tile([P, P], F32)
+
+        def idle_passes(count):
+            for w in range(count):
+                nc.tensor.matmul_mx(
+                    out=idle_sums[:],
+                    lhsT=zero_codes[:].bitcast(FP8X4),
+                    lhsT_scale=zero_scales[:],
+                    rhs=zero_codes[:].bitcast(FP8X4),
+                    rhs_scale=zero_scales[:],
+                    start=(w == 0),
+                    stop=(w == count - 1),
+                )
+
+        idle_passes(WARM_PASSES)
 
         identity = keep.tile([P, P], F32)
         make_identity(nc, identity[:])
         row_zero = keep.tile([P, 2 * OUT_DIM], BF16)
         nc.vector.memset(row_zero[:].bitcast(F32), 0.0)
-
-        warm_zeros = keep.tile([P, PACK * P], BF16, align_bytes=64)
-        nc.vector.memset(warm_zeros[:].bitcast(F32), 0.0)
-        warm_codes = keep.tile([P, P], U32, align_bytes=64)
-        warm_scales = keep.tile([P, P], U8, align_bytes=64)
-        nc.vector.quantize_mx(out=warm_codes[:].bitcast(FP8X4), scales=warm_scales[:], in_=warm_zeros[:])
-        warm_bank = banks.tile([P, WORD_BLOCKS, P], F32, name="bank")
-        for w in range(WARM_PASSES):
-            nc.tensor.matmul_mx(
-                out=warm_bank[:, 0, :],
-                lhsT=warm_codes[:].bitcast(FP8X4),
-                lhsT_scale=warm_scales[:],
-                rhs=warm_codes[:].bitcast(FP8X4),
-                rhs_scale=warm_scales[:],
-                start=(w == 0),
-                stop=(w == WARM_PASSES - 1),
-            )
-
         ones = keep.tile([P, P], BF16)
         nc.vector.memset(ones[:], 1.0)
 
@@ -85,14 +90,19 @@ def tile_doublebinarylinear_s_kernel(tc, x, scaling0, B, scaling2, A, scaling4, 
                 out=s_cols[:].rearrange("p (j e) -> p j e", e=2),
                 in_=scaling.rearrange("(j p e) -> p j e", p=P, e=2),
             )
+        nc.scalar.dma_start(out=row_zero[0:1, 0:OUT_DIM], in_=scaling4.unsqueeze(0))
+        nc.scalar.dma_start(out=row_zero[0:1, OUT_DIM : 2 * OUT_DIM], in_=bias.unsqueeze(0))
         x_sb = keep.tile([P, K_DIM], BF16)
         nc.sync.dma_start(out=x_sb[:], in_=x_rows)
-        nc.sync.dma_start(out=row_zero[0:1, 0:OUT_DIM], in_=scaling4.unsqueeze(0))
-        nc.sync.dma_start(out=row_zero[0:1, OUT_DIM : 2 * OUT_DIM], in_=bias.unsqueeze(0))
         w_sb = []
         for i in range(chunks):
             chunk = keep.tile([P, 2, K_DIM], BF16, name="w_sb%d" % i)
-            nc.sync.dma_start(out=chunk[:], in_=chunk_rows[i].rearrange("(p e) k -> p e k", e=2))
+            rows = chunk_rows[i].rearrange("(p e) k -> p e k", e=2)
+            if i < chunks - 1:
+                nc.sync.dma_start(out=chunk[:], in_=rows)
+            else:
+                for e in range(2):
+                    nc.sync.dma_start(out=chunk[:, e, :], in_=rows[:, e, :])
             w_sb.append(chunk)
 
         x_bank = transpose_row_tile(nc, banks, x_sb[:], identity)
@@ -116,28 +126,21 @@ def tile_doublebinarylinear_s_kernel(tc, x, scaling0, B, scaling2, A, scaling4, 
             in_=h0_grouped[:].rearrange("p g r t -> p (g r t)"),
         )
 
-        s4_bank = banks.tile([P, WORD_BLOCKS, P], F32, name="bank")
-        s4_spread = s4_bank[:].rearrange("p a b -> p (a b)")
-        nc.tensor.matmul(out=s4_spread, lhsT=ones[:], rhs=row_zero[:, 0:OUT_DIM], start=True, stop=True)
-        s4_all = keep.tile([P, OUT_DIM], F32)
-        nc.scalar.copy(out=s4_all[:], in_=s4_spread)
-        bias_all = sums.tile([P, OUT_DIM], F32)
-        nc.tensor.matmul(
-            out=bias_all[:], lhsT=ones[:], rhs=row_zero[:, OUT_DIM : 2 * OUT_DIM], start=True, stop=True
-        )
-
         w_codes = [keep.tile([P, 2, TILE_WORDS], U32, name="w_codes%d" % i, align_bytes=64) for i in range(chunks)]
         w_scales = [keep.tile([P, 2, TILE_WORDS], U8, name="w_scales%d" % i, align_bytes=64) for i in range(chunks)]
         h1 = [sums.tile([P, PACK, P], F32, name="h1_%d" % g, tag="sum%d" % g) for g in range(PASSES)]
         h2_codes = keep.tile([P, TILE_WORDS], U32, align_bytes=64)
         h2_scales = keep.tile([P, TILE_WORDS], U8, align_bytes=64)
 
-        def quantise_chunk(i):
+        def transpose_chunk(i):
+            return [transpose_row_tile(nc, banks, w_sb[i][:, e, :], identity) for e in range(2)]
+
+        def quantise_chunk(i, chunk_banks):
             for e in range(2):
-                bank = transpose_row_tile(nc, banks, w_sb[i][:, e, :], identity)
                 grouped = stage.tile([P, PASSES, P, PACK], BF16, align_bytes=64)
                 nc.scalar.copy(
-                    out=grouped[:].bitcast(F32), in_=bank[:].rearrange("p (g u) r -> p g r u", u=2)
+                    out=grouped[:].bitcast(F32),
+                    in_=chunk_banks[e][:].rearrange("p (g u) r -> p g r u", u=2),
                 )
                 nc.vector.quantize_mx(
                     out=w_codes[i][:, e, :].bitcast(FP8X4),
@@ -197,14 +200,24 @@ def tile_doublebinarylinear_s_kernel(tc, x, scaling0, B, scaling2, A, scaling4, 
             nc.vector.tensor_tensor(out=result[:], in0=result[:], in1=bias_all[:, cols], op=ADD)
             nc.sync.dma_start(out=out_rows[:, cols], in_=result[:])
 
-        def multiply_chunk(i):
-            if i < B_CHUNKS:
-                first_matmul(i)
+        assert chunks - LOOKAHEAD == B_CHUNKS
+        for step in range(chunks):
+            chunk_banks = transpose_chunk(step)
+            if step < LOOKAHEAD:
+                idle_passes(CHUNK_PASSES)
             else:
-                second_matmul(i - B_CHUNKS)
+                first_matmul(step - LOOKAHEAD)
+            quantise_chunk(step, chunk_banks)
 
-        quantise_chunk(0)
-        for i in range(1, chunks):
-            quantise_chunk(i)
-            multiply_chunk(i - 1)
-        multiply_chunk(chunks - 1)
+        s4_bank = banks.tile([P, WORD_BLOCKS, P], F32, name="bank")
+        s4_spread = s4_bank[:].rearrange("p a b -> p (a b)")
+        nc.tensor.matmul(out=s4_spread, lhsT=ones[:], rhs=row_zero[:, 0:OUT_DIM], start=True, stop=True)
+        s4_all = keep.tile([P, OUT_DIM], F32)
+        nc.scalar.copy(out=s4_all[:], in_=s4_spread)
+        bias_all = sums.tile([P, OUT_DIM], F32)
+        nc.tensor.matmul(
+            out=bias_all[:], lhsT=ones[:], rhs=row_zero[:, OUT_DIM : 2 * OUT_DIM], start=True, stop=True
+        )
+
+        for c in range(A_CHUNKS):
+            second_matmul(c)

@@ -21,9 +21,7 @@ CHUNK_ROWS = 2 * P
 B_CHUNKS = 4
 A_CHUNKS = 2
 TILE_WORDS = PASSES * P
-CHUNK_PASSES = 2 * PASSES
 LOOKAHEAD = 2
-WARM_PASSES = 12
 
 FLOPS = 2 * P * K_DIM * K_DIM + 2 * P * K_DIM * OUT_DIM
 
@@ -54,27 +52,6 @@ def tile_doublebinarylinear_s_kernel(tc, x, scaling0, B, scaling2, A, scaling4, 
         banks = ctx.enter_context(tc.psum_pool(name="banks", bufs=4))
         sums = ctx.enter_context(tc.psum_pool(name="sums", bufs=1))
         ctx.enter_context(tc.manual_schedule())
-
-        zeros = keep.tile([P, PACK * P], BF16, align_bytes=64)
-        nc.vector.memset(zeros[:].bitcast(F32), 0.0)
-        zero_codes = keep.tile([P, P], U32, align_bytes=64)
-        zero_scales = keep.tile([P, P], U8, align_bytes=64)
-        nc.vector.quantize_mx(out=zero_codes[:].bitcast(FP8X4), scales=zero_scales[:], in_=zeros[:])
-        idle_sums = sums.tile([P, P], F32)
-
-        def idle_passes(count):
-            for w in range(count):
-                nc.tensor.matmul_mx(
-                    out=idle_sums[:],
-                    lhsT=zero_codes[:].bitcast(FP8X4),
-                    lhsT_scale=zero_scales[:],
-                    rhs=zero_codes[:].bitcast(FP8X4),
-                    rhs_scale=zero_scales[:],
-                    start=(w == 0),
-                    stop=(w == count - 1),
-                )
-
-        idle_passes(WARM_PASSES)
 
         identity = keep.tile([P, P], F32)
         make_identity(nc, identity[:])
@@ -203,9 +180,7 @@ def tile_doublebinarylinear_s_kernel(tc, x, scaling0, B, scaling2, A, scaling4, 
         assert chunks - LOOKAHEAD == B_CHUNKS
         for step in range(chunks):
             chunk_banks = transpose_chunk(step)
-            if step < LOOKAHEAD:
-                idle_passes(CHUNK_PASSES)
-            else:
+            if step >= LOOKAHEAD:
                 first_matmul(step - LOOKAHEAD)
             quantise_chunk(step, chunk_banks)
 

from contextlib import ExitStack

import concourse.mybir as mybir
from concourse.masks import make_identity

BF16 = mybir.dt.bfloat16
F32 = mybir.dt.float32
U32 = mybir.dt.uint32
U8 = mybir.dt.uint8
FP8X4 = mybir.dt.float8_e4m3fn_x4
MULT = mybir.AluOpType.mult
ADD = mybir.AluOpType.add

P = 128
PACK = 4
PASSES = 2
K_DIM = 1024
OUT_DIM = 512
WORD_BLOCKS = 4
CHUNK_ROWS = 2 * P
B_CHUNKS = 4
A_CHUNKS = 2
TILE_WORDS = PASSES * P
LOOKAHEAD = 2

FLOPS = 2 * P * K_DIM * K_DIM + 2 * P * K_DIM * OUT_DIM


def pass_cols(g):
    return slice(g * P, (g + 1) * P)


def transpose_row_tile(nc, banks, rows, identity):
    words = rows.bitcast(F32)
    bank = banks.tile([P, WORD_BLOCKS, P], F32, name="bank")
    for j in range(WORD_BLOCKS):
        nc.tensor.transpose(bank[:, j, :], words[:, j * P : (j + 1) * P], identity[:])
    return bank


def tile_doublebinarylinear_s_kernel(tc, x, scaling0, B, scaling2, A, scaling4, bias, out):
    nc = tc.nc
    x_rows = x.rearrange("b s k -> (b s) k")
    out_rows = out.rearrange("b s o -> (b s) o")
    chunk_rows = [B[c * CHUNK_ROWS : (c + 1) * CHUNK_ROWS, :] for c in range(B_CHUNKS)]
    chunk_rows += [A[c * CHUNK_ROWS : (c + 1) * CHUNK_ROWS, :] for c in range(A_CHUNKS)]
    chunks = len(chunk_rows)

    with ExitStack() as ctx:
        keep = ctx.enter_context(tc.tile_pool(name="keep", bufs=1))
        stage = ctx.enter_context(tc.tile_pool(name="stage", bufs=4))
        banks = ctx.enter_context(tc.psum_pool(name="banks", bufs=4))
        sums = ctx.enter_context(tc.psum_pool(name="sums", bufs=1))
        ctx.enter_context(tc.manual_schedule())

        identity = keep.tile([P, P], F32)
        make_identity(nc, identity[:])
        row_zero = keep.tile([P, 2 * OUT_DIM], BF16)
        nc.vector.memset(row_zero[:].bitcast(F32), 0.0)
        ones = keep.tile([P, P], BF16)
        nc.vector.memset(ones[:], 1.0)

        s0_cols = keep.tile([P, 2 * WORD_BLOCKS], BF16)
        s2_cols = keep.tile([P, 2 * WORD_BLOCKS], BF16)
        for s_cols, scaling in ((s0_cols, scaling0), (s2_cols, scaling2)):
            nc.scalar.dma_start(
                out=s_cols[:].rearrange("p (j e) -> p j e", e=2),
                in_=scaling.rearrange("(j p e) -> p j e", p=P, e=2),
            )
        nc.scalar.dma_start(out=row_zero[0:1, 0:OUT_DIM], in_=scaling4.unsqueeze(0))
        nc.scalar.dma_start(out=row_zero[0:1, OUT_DIM : 2 * OUT_DIM], in_=bias.unsqueeze(0))
        x_sb = keep.tile([P, K_DIM], BF16)
        nc.sync.dma_start(out=x_sb[:], in_=x_rows)
        w_sb = []
        for i in range(chunks):
            chunk = keep.tile([P, 2, K_DIM], BF16, name="w_sb%d" % i)
            rows = chunk_rows[i].rearrange("(p e) k -> p e k", e=2)
            if i < chunks - 1:
                nc.sync.dma_start(out=chunk[:], in_=rows)
            else:
                for e in range(2):
                    nc.sync.dma_start(out=chunk[:, e, :], in_=rows[:, e, :])
            w_sb.append(chunk)

        x_bank = transpose_row_tile(nc, banks, x_sb[:], identity)
        x_halves = x_bank[:].bitcast(BF16)
        h0_grouped = keep.tile([P, PASSES, P, PACK], BF16, align_bytes=64)
        for g in range(PASSES):
            nc.vector.tensor_tensor(
                out=h0_grouped[:, g].rearrange("p r (u e) -> p r u e", e=2),
                in0=x_halves[:, 2 * g : 2 * g + 2, :].rearrange("p u (r e) -> p r u e", e=2),
                in1=s0_cols[:, PACK * g : PACK * (g + 1)]
                .rearrange("p (u e) -> p u e", e=2)
                .unsqueeze(1)
                .to_broadcast([P, P, 2, 2]),
                op=MULT,
            )
        h0_codes = keep.tile([P, TILE_WORDS], U32, align_bytes=64)
        h0_scales = keep.tile([P, TILE_WORDS], U8, align_bytes=64)
        nc.vector.quantize_mx(
            out=h0_codes[:].bitcast(FP8X4),
            scales=h0_scales[:],
            in_=h0_grouped[:].rearrange("p g r t -> p (g r t)"),
        )

        w_codes = [keep.tile([P, 2, TILE_WORDS], U32, name="w_codes%d" % i, align_bytes=64) for i in range(chunks)]
        w_scales = [keep.tile([P, 2, TILE_WORDS], U8, name="w_scales%d" % i, align_bytes=64) for i in range(chunks)]
        h1 = [sums.tile([P, PACK, P], F32, name="h1_%d" % g, tag="sum%d" % g) for g in range(PASSES)]
        h2_codes = keep.tile([P, TILE_WORDS], U32, align_bytes=64)
        h2_scales = keep.tile([P, TILE_WORDS], U8, align_bytes=64)

        def transpose_chunk(i):
            return [transpose_row_tile(nc, banks, w_sb[i][:, e, :], identity) for e in range(2)]

        def quantise_chunk(i, chunk_banks):
            for e in range(2):
                grouped = stage.tile([P, PASSES, P, PACK], BF16, align_bytes=64)
                nc.scalar.copy(
                    out=grouped[:].bitcast(F32),
                    in_=chunk_banks[e][:].rearrange("p (g u) r -> p g r u", u=2),
                )
                nc.vector.quantize_mx(
                    out=w_codes[i][:, e, :].bitcast(FP8X4),
                    scales=w_scales[i][:, e, :],
                    in_=grouped[:].rearrange("p g r t -> p (g r t)"),
                )

        def first_matmul(c):
            g2, u2 = divmod(c, 2)
            for e in range(2):
                for g in range(PASSES):
                    nc.tensor.matmul_mx(
                        out=h1[g2][:, 2 * u2 + e, :],
                        lhsT=w_codes[c][:, e, pass_cols(g)].bitcast(FP8X4),
                        lhsT_scale=w_scales[c][:, e, pass_cols(g)],
                        rhs=h0_codes[:, pass_cols(g)].bitcast(FP8X4),
                        rhs_scale=h0_scales[:, pass_cols(g)],
                        start=(g == 0),
                        stop=(g == PASSES - 1),
                    )
            if u2 == 1:
                h2_grouped = stage.tile([P, P, PACK], BF16, align_bytes=64)
                nc.vector.tensor_tensor(
                    out=h2_grouped[:],
                    in0=h1[g2][:].rearrange("p t r -> p r t"),
                    in1=s2_cols[:, PACK * g2 : PACK * (g2 + 1)].unsqueeze(1).to_broadcast([P, P, PACK]),
                    op=MULT,
                )
                nc.vector.quantize_mx(
                    out=h2_codes[:, pass_cols(g2)].bitcast(FP8X4),
                    scales=h2_scales[:, pass_cols(g2)],
                    in_=h2_grouped[:].rearrange("p r t -> p (r t)"),
                )

        def second_matmul(c):
            i = B_CHUNKS + c
            h3 = sums.tile([P, 2, P], F32, tag="sum%d" % c)
            for e in range(2):
                for g in range(PASSES):
                    nc.tensor.matmul_mx(
                        out=h3[:, e, :],
                        lhsT=h2_codes[:, pass_cols(g)].bitcast(FP8X4),
                        lhsT_scale=h2_scales[:, pass_cols(g)],
                        rhs=w_codes[i][:, e, pass_cols(g)].bitcast(FP8X4),
                        rhs_scale=w_scales[i][:, e, pass_cols(g)],
                        start=(g == 0),
                        stop=(g == PASSES - 1),
                    )
            cols = slice(c * CHUNK_ROWS, (c + 1) * CHUNK_ROWS)
            result = stage.tile([P, CHUNK_ROWS], F32)
            nc.vector.tensor_tensor(
                out=result[:].rearrange("r (p e) -> r p e", e=2),
                in0=h3[:].rearrange("r e p -> r p e"),
                in1=s4_all[:, cols].rearrange("r (p e) -> r p e", e=2),
                op=MULT,
            )
            nc.vector.tensor_tensor(out=result[:], in0=result[:], in1=bias_all[:, cols], op=ADD)
            nc.sync.dma_start(out=out_rows[:, cols], in_=result[:])

        assert chunks - LOOKAHEAD == B_CHUNKS
        for step in range(chunks):
            chunk_banks = transpose_chunk(step)
            if step >= LOOKAHEAD:
                first_matmul(step - LOOKAHEAD)
            quantise_chunk(step, chunk_banks)

        s4_bank = banks.tile([P, WORD_BLOCKS, P], F32, name="bank")
        s4_spread = s4_bank[:].rearrange("p a b -> p (a b)")
        nc.tensor.matmul(out=s4_spread, lhsT=ones[:], rhs=row_zero[:, 0:OUT_DIM], start=True, stop=True)
        s4_all = keep.tile([P, OUT_DIM], F32)
        nc.scalar.copy(out=s4_all[:], in_=s4_spread)
        bias_all = sums.tile([P, OUT_DIM], F32)
        nc.tensor.matmul(
            out=bias_all[:], lhsT=ones[:], rhs=row_zero[:, OUT_DIM : 2 * OUT_DIM], start=True, stop=True
        )

        for c in range(A_CHUNKS):
            second_matmul(c)
